import numpy as np
import ml_dtypes


def mxq(x, axis, fmt="e4m3"):
    dtype, down = {"e4m3": (ml_dtypes.float8_e4m3fn, 7), "e5m2": (ml_dtypes.float8_e5m2, 14)}[fmt]
    v = np.moveaxis(np.asarray(x, np.float32).astype(ml_dtypes.bfloat16).astype(np.float64), axis, -1)
    blocks = v.reshape(v.shape[:-1] + (-1, 32))
    amax = np.abs(blocks).max(-1, keepdims=True)
    byte = np.maximum(np.where(amax > 0, np.frexp(amax)[1] - 1 + 127, 0) - down, 1)
    scale = np.exp2(byte - 127.0)
    codes = (blocks / scale).astype(np.float32).astype(dtype).astype(np.float64)
    return np.moveaxis((codes * scale).reshape(v.shape), -1, axis)


WIDE = False


def mx_kscale(k):
    if not WIDE:
        return np.ones(k)
    levels = np.array([10, -10, 5, -5, 0])
    if k % 512:
        return np.exp2(np.random.permutation(np.resize(levels, k // 32))).repeat(32)
    a = np.empty((k // 512, 16))
    for p in range(k // 512):
        a[p, :8] = np.random.permutation(np.resize(levels, 8))
        for g in range(8):
            far = levels[np.abs(levels - a[p, g]) >= 10]
            a[p, g + 8] = far[np.random.randint(len(far))]
    return np.exp2(a.ravel()).repeat(32)


BF16 = ml_dtypes.bfloat16


def bf(x):
    return np.asarray(x, np.float32).astype(BF16)


def f64(x):
    return np.asarray(x).astype(np.float64)


B, S, E, H, DH, ROT, MP = 4, 2048, 512, 4, 64, 32, 2
HD = H * DH
LOC = HD // MP


def rope_sincos():
    inv_freq = 1.0 / (10000.0 ** (np.arange(0, ROT, 2) / ROT))
    ang = np.arange(S)[:, None] * inv_freq[None, :]
    return np.sin(ang), np.cos(ang)


def apply_rope(x, sin, cos):
    sin2 = np.repeat(sin, 2, axis=-1)[None, :, None, :]
    cos2 = np.repeat(cos, 2, axis=-1)[None, :, None, :]
    x1 = x[..., ::2]
    x2 = x[..., 1::2]
    rot = np.stack((-x2, x1), axis=-1).reshape(x.shape)
    return x * cos2 + rot * sin2


def setup_inputs():
    s = mx_kscale(E)
    return {"hidden_states": bf(np.random.standard_normal((B, S, E)) * s),
            "W_qkv": bf(np.random.standard_normal((3 * HD, E)) / np.sqrt(E) / s[None, :])}


def reference(hidden_states, W_qkv):
    qkv = mxq(f64(hidden_states), 2, "e4m3") @ mxq(f64(W_qkv).T, 0, "e4m3")
    qkv = qkv.reshape(B, S, MP, 3 * LOC)
    q, k, v = np.split(qkv, 3, axis=-1)
    q = q.reshape(B, S, H, DH)
    k = k.reshape(B, S, H, DH)
    v = v.reshape(B, S, H, DH)
    sin, cos = rope_sincos()
    q = np.concatenate([apply_rope(q[..., :ROT], sin, cos), q[..., ROT:]], axis=-1)
    k = np.concatenate([apply_rope(k[..., :ROT], sin, cos), k[..., ROT:]], axis=-1)
    return q, k, v

@@ -1,0 +1,287 @@
+import math
+from contextlib import ExitStack
+
+import concourse.mybir as mybir
+from concourse.masks import make_identity
+
+F32 = mybir.dt.float32
+BF16 = mybir.dt.bfloat16
+I32 = mybir.dt.int32
+U32 = mybir.dt.uint32
+U8 = mybir.dt.uint8
+FP8X4 = mybir.dt.float8_e4m3fn_x4
+ALU = mybir.AluOpType
+ACT = mybir.ActivationFunctionType
+
+P = 128
+B, S, E = 4, 2048, 512
+H, DH, ROT = 4, 64, 32
+HD = H * DH
+GROUPS = 2
+ANGLES = ROT // 2
+POS_PER_PART = S // P
+WORDS = E // 2
+CHUNK = 4
+CHUNKS = POS_PER_PART // CHUNK
+ROUND_MAGIC = 12582912.0
+
+FLOPS = 2 * B * S * E * 3 * HD
+
+
+def build_rope_tables(nc, pool, tables):
+    turns_per_position = [
+        1.0 / (2.0 * math.pi * 10000.0 ** (2.0 * j / ROT)) for j in range(ANGLES)
+    ]
+    g_hi = [round(g * 32768.0) / 32768.0 for g in turns_per_position]
+    g_lo = [g - hi for g, hi in zip(turns_per_position, g_hi)]
+
+    position_int = pool.tile([P, POS_PER_PART], I32)
+    nc.gpsimd.iota(
+        position_int[:], pattern=[[1, POS_PER_PART]], base=0, channel_multiplier=POS_PER_PART
+    )
+    position = pool.tile([P, POS_PER_PART], F32)
+    nc.vector.tensor_copy(out=position[:], in_=position_int[:])
+
+    coarse = pool.tile([P, POS_PER_PART, ANGLES], F32)
+    for j in range(ANGLES):
+        nc.vector.tensor_scalar(
+            out=coarse[:, :, j], in0=position[:], scalar1=g_hi[j], scalar2=None, op0=ALU.mult
+        )
+    coarse_integer = pool.tile([P, POS_PER_PART, ANGLES], F32)
+    nc.vector.tensor_scalar(
+        out=coarse_integer[:],
+        in0=coarse[:],
+        scalar1=ROUND_MAGIC,
+        scalar2=ROUND_MAGIC,
+        op0=ALU.add,
+        op1=ALU.subtract,
+    )
+    nc.vector.tensor_tensor(
+        out=coarse[:], in0=coarse[:], in1=coarse_integer[:], op=ALU.subtract
+    )
+    turns = pool.tile([P, POS_PER_PART, ANGLES], F32)
+    for j in range(ANGLES):
+        nc.vector.scalar_tensor_tensor(
+            out=turns[:, :, j],
+            in0=position[:],
+            scalar=g_lo[j],
+            in1=coarse[:, :, j],
+            op0=ALU.mult,
+            op1=ALU.add,
+        )
+
+    argument = pool.tile([P, 2, POS_PER_PART, ANGLES, 2], F32)
+    nc.vector.tensor_scalar_add(out=argument[:, 0, :, :, 0], in0=turns[:], scalar1=0.25)
+    nc.vector.tensor_copy(out=argument[:, 0, :, :, 1], in_=turns[:])
+    nc.vector.tensor_scalar_mul(out=argument[:, 1, :, :, 0], in0=turns[:], scalar1=-1.0)
+    nc.vector.tensor_scalar_add(out=argument[:, 1, :, :, 1], in0=turns[:], scalar1=0.25)
+    flat_argument = argument[:].rearrange("p k i j e -> p (k i j e)")
+    argument_integer = pool.tile([P, 2 * POS_PER_PART * ROT], F32)
+    nc.vector.tensor_scalar(
+        out=argument_integer[:],
+        in0=flat_argument,
+        scalar1=ROUND_MAGIC,
+        scalar2=ROUND_MAGIC,
+        op0=ALU.add,
+        op1=ALU.subtract,
+    )
+    nc.vector.tensor_tensor(
+        out=flat_argument, in0=flat_argument, in1=argument_integer[:], op=ALU.subtract
+    )
+    nc.scalar.activation(
+        out=tables[:].rearrange("p k i c -> p (k i c)"),
+        in_=flat_argument,
+        func=ACT.Sin,
+        scale=2.0 * math.pi,
+    )
+
+
+def tile_progenattention_pa_t_kernel(tc, hidden_states, W_qkv, out_0, out_1, out_2):
+    nc = tc.nc
+    with ExitStack() as ctx:
+        const = ctx.enter_context(tc.tile_pool(name="const", bufs=1))
+        x_pool = ctx.enter_context(tc.tile_pool(name="x_pool", bufs=B * CHUNKS))
+        operand_pool = ctx.enter_context(tc.tile_pool(name="operand_pool", bufs=3))
+        stage_pool = ctx.enter_context(tc.tile_pool(name="stage_pool", bufs=4))
+        psum = ctx.enter_context(tc.psum_pool(name="psum", bufs=2))
+
+        x_rows = [hidden_states[b].rearrange("(p i) k -> p (i k)", i=POS_PER_PART) for b in range(B)]
+        out_rows = [
+            [out[b].rearrange("(p i) h d -> p (i h d)", i=POS_PER_PART) for b in range(B)]
+            for out in (out_0, out_1, out_2)
+        ]
+
+        pairs = [
+            (bc, chunk, t) for bc in range(B // 2) for chunk in range(CHUNKS) for t in range(CHUNK)
+        ]
+
+        w_rows = const.tile([P, 3 * GROUPS, E], BF16)
+        nc.sync.dma_start(out=w_rows[:], in_=W_qkv.rearrange("(a p) k -> p a k", p=P))
+        x_chunks = {}
+        for bc in range(B // 2):
+            for chunk in range(CHUNKS):
+                for side in range(2):
+                    x_chunk = x_pool.tile([P, CHUNK * E], BF16)
+                    nc.sync.dma_start(
+                        out=x_chunk[:],
+                        in_=x_rows[2 * bc + side][:, chunk * CHUNK * E : (chunk + 1) * CHUNK * E],
+                    )
+                    x_chunks[(bc, chunk, side)] = x_chunk
+
+        warm_in = const.tile([P, 1], F32)
+        warm_out = const.tile([P, 1], F32)
+        nc.vector.memset(warm_in[:], 0.0)
+        nc.scalar.activation(out=warm_out[:], in_=warm_in[:], func=ACT.Sin)
+
+        tables = const.tile([P, 2, POS_PER_PART, ROT], F32)
+        build_rope_tables(nc, const, tables)
+
+        identity = const.tile([P, P], F32)
+        make_identity(nc, identity[:])
+
+        w_grouped = const.tile([P, 3 * HD * 4], BF16, align_bytes=64)
+        w_words = w_grouped[:].bitcast(F32).rearrange("p (c u) -> p c u", u=2)
+        w_codes = const.tile([P, 3 * HD], U32, align_bytes=64)
+        w_scales = const.tile([P, 3 * HD], U8, align_bytes=64)
+        for kind in range(3):
+            w_t = psum.tile([P, 2, 2, P], F32, name="transposed")
+            for g in range(GROUPS):
+                words = w_rows[:, 3 * g + kind, :].bitcast(F32)
+                for u in range(2):
+                    nc.tensor.transpose(w_t[:, g, u, :], words[:, u:WORDS:2], identity[:])
+            if kind == 2:
+                nc.scalar.copy(
+                    out=w_words[:, 2 * HD : 3 * HD, :].rearrange("p (g r) u -> p g r u", g=GROUPS),
+                    in_=w_t[:].rearrange("p g u r -> p g r u"),
+                )
+            else:
+                halves = w_t[:].rearrange("p g u (hh f d) -> p g f hh d u", hh=2, f=2)
+                for f in range(2):
+                    for g in range(GROUPS):
+                        first = f * HD + kind * (HD // 2) + g * 2 * ROT
+                        nc.scalar.copy(
+                            out=w_words[:, first : first + 2 * ROT, :].rearrange(
+                                "p (hh d) u -> p hh d u", hh=2
+                            ),
+                            in_=halves[:, g, f, :, :, :],
+                        )
+        for block in range(3):
+            nc.vector.quantize_mx(
+                out=w_codes[:, block * HD : (block + 1) * HD].bitcast(FP8X4),
+                scales=w_scales[:, block * HD : (block + 1) * HD],
+                in_=w_grouped[:, block * HD * 4 : (block + 1) * HD * 4],
+            )
+
+        def transpose_pair(bc, chunk, t):
+            transposed = psum.tile([P, 2, 2, P], F32, name="transposed")
+            for side in range(2):
+                words = x_chunks[(bc, chunk, side)][:].bitcast(F32)
+                for u in range(2):
+                    first = t * WORDS + u
+                    nc.tensor.transpose(
+                        transposed[:, side, u, :],
+                        words[:, first : (t + 1) * WORDS : 2],
+                        identity[:],
+                    )
+            grouped = operand_pool.tile([P, 2 * E], BF16, align_bytes=64)
+            nc.scalar.copy(
+                out=grouped[:].bitcast(F32).rearrange("p (b r u) -> p b r u", b=2, u=2),
+                in_=transposed[:].rearrange("p b u r -> p b r u"),
+            )
+            return grouped
+
+        def quantise_pair(grouped):
+            codes = operand_pool.tile([P, 2 * P], U32, align_bytes=64)
+            scales = operand_pool.tile([P, 2 * P], U8, align_bytes=64)
+            nc.vector.quantize_mx(out=codes[:].bitcast(FP8X4), scales=scales[:], in_=grouped[:])
+            return codes, scales
+
+        def project_pair(codes, scales, qk_stage, v_stage, i, t):
+            rotated_ps = psum.tile([P, 2 * HD], F32)
+            passing_ps = psum.tile([P, 2 * HD], F32)
+            v_ps = psum.tile([P, 2 * HD], F32)
+            for block, bank in enumerate((rotated_ps, passing_ps, v_ps)):
+                for side in range(2):
+                    nc.tensor.matmul_mx(
+                        out=bank[:, side * HD : (side + 1) * HD],
+                        lhsT=codes[:, side * P : (side + 1) * P].bitcast(FP8X4),
+                        lhsT_scale=scales[:, side * P : (side + 1) * P],
+                        rhs=w_codes[:, block * HD : (block + 1) * HD].bitcast(FP8X4),
+                        rhs_scale=w_scales[:, block * HD : (block + 1) * HD],
+                        start=True,
+                        stop=True,
+                    )
+            shape = [P, 4, H, ANGLES, 2]
+            couples = rotated_ps[:].rearrange("p (c h j e) -> p c h j e", c=4, h=H, e=2)
+            spread = [
+                tables[:, k, i, :]
+                .rearrange("p (j e) -> p j e", e=2)
+                .unsqueeze(1)
+                .unsqueeze(1)
+                .to_broadcast(shape)
+                for k in range(2)
+            ]
+            rotated_out = qk_stage[:].rearrange(
+                "p b s (t h j e) -> p (b s) t h j e", t=CHUNK, h=H, e=2
+            )[:, :, t, :, 0:ANGLES, :]
+            nc.vector.tensor_tensor(
+                out=rotated_out,
+                in0=couples[:, :, :, :, 0:1].to_broadcast(shape),
+                in1=spread[0],
+                op=ALU.mult,
+            )
+            odd_product = operand_pool.tile([P, 2 * HD], F32)
+            odd_view = odd_product[:].rearrange("p (c h j e) -> p c h j e", c=4, h=H, e=2)
+            nc.vector.tensor_tensor(
+                out=odd_view,
+                in0=couples[:, :, :, :, 1:2].to_broadcast(shape),
+                in1=spread[1],
+                op=ALU.mult,
+            )
+            nc.scalar.copy(
+                out=qk_stage[:].rearrange("p b s (t h d) -> p (b s) t h d", t=CHUNK, h=H)[
+                    :, :, t, :, ROT:DH
+                ],
+                in_=passing_ps[:].rearrange("p (c h d) -> p c h d", c=4, h=H),
+            )
+            nc.scalar.copy(
+                out=v_stage[:, :, t * HD : (t + 1) * HD],
+                in_=v_ps[:].rearrange("p (b n) -> p b n", b=2),
+            )
+            return rotated_out, odd_view
+
+        def finish_pair(rotated_out, odd_view):
+            nc.vector.tensor_tensor(out=rotated_out, in0=rotated_out, in1=odd_view, op=ALU.add)
+
+        def store_chunk(bc, chunk, qk_stage, v_stage):
+            columns = slice(chunk * CHUNK * HD, (chunk + 1) * CHUNK * HD)
+            for side in range(2):
+                b = 2 * bc + side
+                nc.sync.dma_start(out=out_rows[2][b][:, columns], in_=v_stage[:, side, :])
+                nc.sync.dma_start(out=out_rows[0][b][:, columns], in_=qk_stage[:, side, 0, :])
+                nc.sync.dma_start(out=out_rows[1][b][:, columns], in_=qk_stage[:, side, 1, :])
+
+        grouped_of = {}
+        operand_of = {}
+        stage_of = {}
+        products_of = {}
+        for n in range(len(pairs) + 3):
+            if n < len(pairs):
+                grouped_of[n] = transpose_pair(*pairs[n])
+            if 0 <= n - 1 < len(pairs):
+                operand_of[n - 1] = quantise_pair(grouped_of[n - 1])
+            if 0 <= n - 2 < len(pairs):
+                bc, chunk, t = pairs[n - 2]
+                if t == 0:
+                    qk_stage = stage_pool.tile([P, 2, 2, CHUNK * HD], F32)
+                    v_stage = stage_pool.tile([P, 2, CHUNK * HD], F32)
+                    stage_of[(bc, chunk)] = (qk_stage, v_stage)
+                codes, scales = operand_of[n - 2]
+                products_of[n - 2] = project_pair(
+                    codes, scales, *stage_of[(bc, chunk)], chunk * CHUNK + t, t
+                )
+            if 0 <= n - 3:
+                bc, chunk, t = pairs[n - 3]
+                finish_pair(*products_of[n - 3])
+                if t == CHUNK - 1:
+                    store_chunk(bc, chunk, *stage_of[(bc, chunk)])

@@ -21,8 +21,10 @@ GROUPS = 2
 ANGLES = ROT // 2
 POS_PER_PART = S // P
 WORDS = E // 2
-CHUNK = 4
-CHUNKS = POS_PER_PART // CHUNK
+PAIRS = POS_PER_PART // 2
+LOAD_SIZES = [[2, 6, 8], [16], [16], [16]]
+STORE_SIZES = [[8, 8], [8, 8], [8, 8], [8, 4, 2, 2]]
+MAX_STORE = max(max(sizes) for sizes in STORE_SIZES)
 ROUND_MAGIC = 12582912.0
 
 FLOPS = 2 * B * S * E * 3 * HD
@@ -70,12 +72,13 @@ def build_rope_tables(nc, pool, tables):
             op1=ALU.add,
         )
 
-    argument = pool.tile([P, 2, POS_PER_PART, ANGLES, 2], F32)
-    nc.vector.tensor_scalar_add(out=argument[:, 0, :, :, 0], in0=turns[:], scalar1=0.25)
-    nc.vector.tensor_copy(out=argument[:, 0, :, :, 1], in_=turns[:])
-    nc.vector.tensor_scalar_mul(out=argument[:, 1, :, :, 0], in0=turns[:], scalar1=-1.0)
-    nc.vector.tensor_scalar_add(out=argument[:, 1, :, :, 1], in0=turns[:], scalar1=0.25)
-    flat_argument = argument[:].rearrange("p k i j e -> p (k i j e)")
+    argument = pool.tile([P, PAIRS, 2, 2, ANGLES, 2], F32)
+    paired = turns[:].rearrange("p (m s) j -> p m s j", s=2)
+    nc.vector.tensor_scalar_add(out=argument[:, :, 0, :, :, 0], in0=paired, scalar1=0.25)
+    nc.vector.tensor_copy(out=argument[:, :, 0, :, :, 1], in_=paired)
+    nc.vector.tensor_scalar_mul(out=argument[:, :, 1, :, :, 0], in0=paired, scalar1=-1.0)
+    nc.vector.tensor_scalar_add(out=argument[:, :, 1, :, :, 1], in0=paired, scalar1=0.25)
+    flat_argument = argument[:].rearrange("p m k s j e -> p (m k s j e)")
     argument_integer = pool.tile([P, 2 * POS_PER_PART * ROT], F32)
     nc.vector.tensor_scalar(
         out=argument_integer[:],
@@ -89,7 +92,7 @@ def build_rope_tables(nc, pool, tables):
         out=flat_argument, in0=flat_argument, in1=argument_integer[:], op=ALU.subtract
     )
     nc.scalar.activation(
-        out=tables[:].rearrange("p k i c -> p (k i c)"),
+        out=tables[:].rearrange("p m k s c -> p (m k s c)"),
         in_=flat_argument,
         func=ACT.Sin,
         scale=2.0 * math.pi,
@@ -100,7 +103,7 @@ def tile_progenattention_pa_t_kernel(tc, hidden_states, W_qkv, out_0, out_1, out
     nc = tc.nc
     with ExitStack() as ctx:
         const = ctx.enter_context(tc.tile_pool(name="const", bufs=1))
-        x_pool = ctx.enter_context(tc.tile_pool(name="x_pool", bufs=B * CHUNKS))
+        x_pool = ctx.enter_context(tc.tile_pool(name="x_pool", bufs=1))
         operand_pool = ctx.enter_context(tc.tile_pool(name="operand_pool", bufs=3))
         stage_pool = ctx.enter_context(tc.tile_pool(name="stage_pool", bufs=4))
         psum = ctx.enter_context(tc.psum_pool(name="psum", bufs=2))
@@ -111,29 +114,35 @@ def tile_progenattention_pa_t_kernel(tc, hidden_states, W_qkv, out_0, out_1, out
             for out in (out_0, out_1, out_2)
         ]
 
-        pairs = [
-            (bc, chunk, t) for bc in range(B // 2) for chunk in range(CHUNKS) for t in range(CHUNK)
-        ]
+        pairs = [(b, m) for b in range(B) for m in range(PAIRS)]
+        store_run = {}
+        for b in range(B):
+            first = 0
+            for size in STORE_SIZES[b]:
+                for m in range(first // 2, (first + size) // 2):
+                    store_run[(b, m)] = (first, size)
+                first += size
 
         w_rows = const.tile([P, 3 * GROUPS, E], BF16)
         nc.sync.dma_start(out=w_rows[:], in_=W_qkv.rearrange("(a p) k -> p a k", p=P))
-        x_chunks = {}
-        for bc in range(B // 2):
-            for chunk in range(CHUNKS):
-                for side in range(2):
-                    x_chunk = x_pool.tile([P, CHUNK * E], BF16)
-                    nc.sync.dma_start(
-                        out=x_chunk[:],
-                        in_=x_rows[2 * bc + side][:, chunk * CHUNK * E : (chunk + 1) * CHUNK * E],
-                    )
-                    x_chunks[(bc, chunk, side)] = x_chunk
+        x_words = {}
+        for b in range(B):
+            first = 0
+            for size in LOAD_SIZES[b]:
+                x_run = x_pool.tile([P, size * E], BF16, name="x_%d_%d" % (b, first))
+                nc.sync.dma_start(
+                    out=x_run[:], in_=x_rows[b][:, first * E : (first + size) * E]
+                )
+                for i in range(size):
+                    x_words[(b, first + i)] = x_run[:].bitcast(F32)[:, i * WORDS : (i + 1) * WORDS]
+                first += size
 
         warm_in = const.tile([P, 1], F32)
         warm_out = const.tile([P, 1], F32)
         nc.vector.memset(warm_in[:], 0.0)
         nc.scalar.activation(out=warm_out[:], in_=warm_in[:], func=ACT.Sin)
 
-        tables = const.tile([P, 2, POS_PER_PART, ROT], F32)
+        tables = const.tile([P, PAIRS, 2, 2, ROT], F32)
         build_rope_tables(nc, const, tables)
 
         identity = const.tile([P, P], F32)
@@ -172,21 +181,18 @@ def tile_progenattention_pa_t_kernel(tc, hidden_states, W_qkv, out_0, out_1, out
                 in_=w_grouped[:, block * HD * 4 : (block + 1) * HD * 4],
             )
 
-        def transpose_pair(bc, chunk, t):
+        def transpose_pair(b, m):
             transposed = psum.tile([P, 2, 2, P], F32, name="transposed")
             for side in range(2):
-                words = x_chunks[(bc, chunk, side)][:].bitcast(F32)
+                words = x_words[(b, 2 * m + side)]
                 for u in range(2):
-                    first = t * WORDS + u
                     nc.tensor.transpose(
-                        transposed[:, side, u, :],
-                        words[:, first : (t + 1) * WORDS : 2],
-                        identity[:],
+                        transposed[:, side, u, :], words[:, u:WORDS:2], identity[:]
                     )
             grouped = operand_pool.tile([P, 2 * E], BF16, align_bytes=64)
             nc.scalar.copy(
-                out=grouped[:].bitcast(F32).rearrange("p (b r u) -> p b r u", b=2, u=2),
-                in_=transposed[:].rearrange("p b u r -> p b r u"),
+                out=grouped[:].bitcast(F32).rearrange("p (s r u) -> p s r u", s=2, u=2),
+                in_=transposed[:].rearrange("p s u r -> p s r u"),
             )
             return grouped
 
@@ -196,7 +202,7 @@ def tile_progenattention_pa_t_kernel(tc, hidden_states, W_qkv, out_0, out_1, out
             nc.vector.quantize_mx(out=codes[:].bitcast(FP8X4), scales=scales[:], in_=grouped[:])
             return codes, scales
 
-        def project_pair(codes, scales, qk_stage, v_stage, i, t):
+        def project_pair(codes, scales, qk_stage, v_stage, m, t):
             rotated_ps = psum.tile([P, 2 * HD], F32)
             passing_ps = psum.tile([P, 2 * HD], F32)
             v_ps = psum.tile([P, 2 * HD], F32)
@@ -211,55 +217,45 @@ def tile_progenattention_pa_t_kernel(tc, hidden_states, W_qkv, out_0, out_1, out
                         start=True,
                         stop=True,
                     )
-            shape = [P, 4, H, ANGLES, 2]
-            couples = rotated_ps[:].rearrange("p (c h j e) -> p c h j e", c=4, h=H, e=2)
-            spread = [
-                tables[:, k, i, :]
-                .rearrange("p (j e) -> p j e", e=2)
-                .unsqueeze(1)
-                .unsqueeze(1)
-                .to_broadcast(shape)
-                for k in range(2)
-            ]
-            rotated_out = qk_stage[:].rearrange(
-                "p b s (t h j e) -> p (b s) t h j e", t=CHUNK, h=H, e=2
-            )[:, :, t, :, 0:ANGLES, :]
+            products = operand_pool.tile([P, 2, 2 * HD], F32)
+            shape = [P, 2, 2, 2 * H, ANGLES, 2]
             nc.vector.tensor_tensor(
-                out=rotated_out,
-                in0=couples[:, :, :, :, 0:1].to_broadcast(shape),
-                in1=spread[0],
-                op=ALU.mult,
-            )
-            odd_product = operand_pool.tile([P, 2 * HD], F32)
-            odd_view = odd_product[:].rearrange("p (c h j e) -> p c h j e", c=4, h=H, e=2)
-            nc.vector.tensor_tensor(
-                out=odd_view,
-                in0=couples[:, :, :, :, 1:2].to_broadcast(shape),
-                in1=spread[1],
+                out=products[:].rearrange("p k (s c j e) -> p k s c j e", s=2, c=2 * H, e=2),
+                in0=rotated_ps[:]
+                .rearrange("p (s c j k) -> p k s c j", s=2, c=2 * H, k=2)
+                .unsqueeze(5)
+                .to_broadcast(shape),
+                in1=tables[:, m, :, :, :]
+                .rearrange("p k s (j e) -> p k s j e", e=2)
+                .unsqueeze(3)
+                .to_broadcast(shape),
                 op=ALU.mult,
             )
             nc.scalar.copy(
-                out=qk_stage[:].rearrange("p b s (t h d) -> p (b s) t h d", t=CHUNK, h=H)[
-                    :, :, t, :, ROT:DH
-                ],
-                in_=passing_ps[:].rearrange("p (c h d) -> p c h d", c=4, h=H),
+                out=qk_stage[:, :, t * HD : (t + 2) * HD].rearrange(
+                    "p c (s h d) -> p c s h d", s=2, h=H
+                )[:, :, :, :, ROT:DH],
+                in_=passing_ps[:].rearrange("p (s c h d) -> p c s h d", s=2, c=2, h=H),
             )
-            nc.scalar.copy(
-                out=v_stage[:, :, t * HD : (t + 1) * HD],
-                in_=v_ps[:].rearrange("p (b n) -> p b n", b=2),
+            nc.scalar.copy(out=v_stage[:, t * HD : (t + 2) * HD], in_=v_ps[:])
+            return products
+
+        def finish_pair(products, qk_stage, t):
+            terms = products[:].rearrange("p k (s c h d) -> p k c s h d", s=2, c=2, h=H)
+            nc.vector.tensor_tensor(
+                out=qk_stage[:, :, t * HD : (t + 2) * HD].rearrange(
+                    "p c (s h d) -> p c s h d", s=2, h=H
+                )[:, :, :, :, 0:ROT],
+                in0=terms[:, 0, :, :, :, :],
+                in1=terms[:, 1, :, :, :, :],
+                op=ALU.add,
             )
-            return rotated_out, odd_view
 
-        def finish_pair(rotated_out, odd_view):
-            nc.vector.tensor_tensor(out=rotated_out, in0=rotated_out, in1=odd_view, op=ALU.add)
-
-        def store_chunk(bc, chunk, qk_stage, v_stage):
-            columns = slice(chunk * CHUNK * HD, (chunk + 1) * CHUNK * HD)
-            for side in range(2):
-                b = 2 * bc + side
-                nc.sync.dma_start(out=out_rows[2][b][:, columns], in_=v_stage[:, side, :])
-                nc.sync.dma_start(out=out_rows[0][b][:, columns], in_=qk_stage[:, side, 0, :])
-                nc.sync.dma_start(out=out_rows[1][b][:, columns], in_=qk_stage[:, side, 1, :])
+        def store(b, first, size, qk_stage, v_stage):
+            columns = slice(first * HD, (first + size) * HD)
+            nc.sync.dma_start(out=out_rows[2][b][:, columns], in_=v_stage[:, 0 : size * HD])
+            nc.sync.dma_start(out=out_rows[0][b][:, columns], in_=qk_stage[:, 0, 0 : size * HD])
+            nc.sync.dma_start(out=out_rows[1][b][:, columns], in_=qk_stage[:, 1, 0 : size * HD])
 
         grouped_of = {}
         operand_of = {}
@@ -271,17 +267,20 @@ def tile_progenattention_pa_t_kernel(tc, hidden_states, W_qkv, out_0, out_1, out
             if 0 <= n - 1 < len(pairs):
                 operand_of[n - 1] = quantise_pair(grouped_of[n - 1])
             if 0 <= n - 2 < len(pairs):
-                bc, chunk, t = pairs[n - 2]
-                if t == 0:
-                    qk_stage = stage_pool.tile([P, 2, 2, CHUNK * HD], F32)
-                    v_stage = stage_pool.tile([P, 2, CHUNK * HD], F32)
-                    stage_of[(bc, chunk)] = (qk_stage, v_stage)
+                b, m = pairs[n - 2]
+                first, size = store_run[(b, m)]
+                if 2 * m == first:
+                    qk_stage = stage_pool.tile([P, 2, MAX_STORE * HD], F32)
+                    v_stage = stage_pool.tile([P, MAX_STORE * HD], F32)
+                    stage_of[(b, first)] = (qk_stage, v_stage)
                 codes, scales = operand_of[n - 2]
                 products_of[n - 2] = project_pair(
-                    codes, scales, *stage_of[(bc, chunk)], chunk * CHUNK + t, t
+                    codes, scales, *stage_of[(b, first)], m, 2 * m - first
                 )
             if 0 <= n - 3:
-                bc, chunk, t = pairs[n - 3]
-                finish_pair(*products_of[n - 3])
-                if t == CHUNK - 1:
-                    store_chunk(bc, chunk, *stage_of[(bc, chunk)])
+                b, m = pairs[n - 3]
+                first, size = store_run[(b, m)]
+                qk_stage, v_stage = stage_of[(b, first)]
+                finish_pair(products_of[n - 3], qk_stage, 2 * m - first)
+                if 2 * m + 2 == first + size:
+                    store(b, first, size, qk_stage, v_stage)

@@ -6,7 +6,6 @@ from concourse.masks import make_identity
 
 F32 = mybir.dt.float32
 BF16 = mybir.dt.bfloat16
-I32 = mybir.dt.int32
 U32 = mybir.dt.uint32
 U8 = mybir.dt.uint8
 FP8X4 = mybir.dt.float8_e4m3fn_x4
@@ -37,63 +36,58 @@ def build_rope_tables(nc, pool, tables):
     g_hi = [round(g * 32768.0) / 32768.0 for g in turns_per_position]
     g_lo = [g - hi for g, hi in zip(turns_per_position, g_hi)]
 
-    position_int = pool.tile([P, POS_PER_PART], I32)
-    nc.gpsimd.iota(
-        position_int[:], pattern=[[1, POS_PER_PART]], base=0, channel_multiplier=POS_PER_PART
-    )
     position = pool.tile([P, POS_PER_PART], F32)
-    nc.vector.tensor_copy(out=position[:], in_=position_int[:])
+    nc.gpsimd.iota(
+        position[:],
+        pattern=[[1, POS_PER_PART]],
+        base=0,
+        channel_multiplier=POS_PER_PART,
+        allow_small_or_imprecise_dtypes=True,
+    )
 
     coarse = pool.tile([P, POS_PER_PART, ANGLES], F32)
+    fine = pool.tile([P, POS_PER_PART, ANGLES], F32)
     for j in range(ANGLES):
         nc.vector.tensor_scalar(
             out=coarse[:, :, j], in0=position[:], scalar1=g_hi[j], scalar2=None, op0=ALU.mult
         )
-    coarse_integer = pool.tile([P, POS_PER_PART, ANGLES], F32)
-    nc.vector.tensor_scalar(
-        out=coarse_integer[:],
-        in0=coarse[:],
-        scalar1=ROUND_MAGIC,
-        scalar2=ROUND_MAGIC,
-        op0=ALU.add,
-        op1=ALU.subtract,
-    )
-    nc.vector.tensor_tensor(
-        out=coarse[:], in0=coarse[:], in1=coarse_integer[:], op=ALU.subtract
-    )
-    turns = pool.tile([P, POS_PER_PART, ANGLES], F32)
-    for j in range(ANGLES):
-        nc.vector.scalar_tensor_tensor(
-            out=turns[:, :, j],
-            in0=position[:],
-            scalar=g_lo[j],
-            in1=coarse[:, :, j],
-            op0=ALU.mult,
-            op1=ALU.add,
-        )
+        nc.scalar.activation(out=fine[:, :, j], in_=position[:], func=ACT.Copy, scale=g_lo[j])
+    nearest = pool.tile([P, POS_PER_PART, ANGLES], F32)
 
+    def to_nearest_integer(values):
+        nc.vector.tensor_scalar(
+            out=nearest[:],
+            in0=values[:],
+            scalar1=ROUND_MAGIC,
+            scalar2=ROUND_MAGIC,
+            op0=ALU.add,
+            op1=ALU.subtract,
+        )
+        nc.vector.tensor_tensor(out=values[:], in0=values[:], in1=nearest[:], op=ALU.subtract)
+
+    to_nearest_integer(coarse)
+    turns = pool.tile([P, POS_PER_PART, ANGLES], F32)
+    nc.vector.tensor_tensor(out=turns[:], in0=coarse[:], in1=fine[:], op=ALU.add)
+    to_nearest_integer(turns)
+
+    above = pool.tile([P, POS_PER_PART, ANGLES], F32)
+    nc.vector.tensor_scalar(
+        out=above[:], in0=turns[:], scalar1=0.25, scalar2=None, op0=ALU.is_gt
+    )
     argument = pool.tile([P, PAIRS, 2, 2, ANGLES, 2], F32)
     paired = turns[:].rearrange("p (m s) j -> p m s j", s=2)
-    nc.vector.tensor_scalar_add(out=argument[:, :, 0, :, :, 0], in0=paired, scalar1=0.25)
+    shifted = pool.tile([P, POS_PER_PART, ANGLES], F32)
+    nc.vector.scalar_tensor_tensor(
+        out=shifted[:], in0=turns[:], scalar=0.25, in1=above[:], op0=ALU.add, op1=ALU.subtract
+    )
+    paired_shifted = shifted[:].rearrange("p (m s) j -> p m s j", s=2)
+    nc.vector.tensor_copy(out=argument[:, :, 0, :, :, 0], in_=paired_shifted)
     nc.vector.tensor_copy(out=argument[:, :, 0, :, :, 1], in_=paired)
     nc.vector.tensor_scalar_mul(out=argument[:, :, 1, :, :, 0], in0=paired, scalar1=-1.0)
-    nc.vector.tensor_scalar_add(out=argument[:, :, 1, :, :, 1], in0=paired, scalar1=0.25)
-    flat_argument = argument[:].rearrange("p m k s j e -> p (m k s j e)")
-    argument_integer = pool.tile([P, 2 * POS_PER_PART * ROT], F32)
-    nc.vector.tensor_scalar(
-        out=argument_integer[:],
-        in0=flat_argument,
-        scalar1=ROUND_MAGIC,
-        scalar2=ROUND_MAGIC,
-        op0=ALU.add,
-        op1=ALU.subtract,
-    )
-    nc.vector.tensor_tensor(
-        out=flat_argument, in0=flat_argument, in1=argument_integer[:], op=ALU.subtract
-    )
+    nc.vector.tensor_copy(out=argument[:, :, 1, :, :, 1], in_=paired_shifted)
     nc.scalar.activation(
         out=tables[:].rearrange("p m k s c -> p (m k s c)"),
-        in_=flat_argument,
+        in_=argument[:].rearrange("p m k s j e -> p (m k s j e)"),
         func=ACT.Sin,
         scale=2.0 * math.pi,
     )
@@ -123,18 +117,32 @@ def tile_progenattention_pa_t_kernel(tc, hidden_states, W_qkv, out_0, out_1, out
                     store_run[(b, m)] = (first, size)
                 first += size
 
-        w_rows = const.tile([P, 3 * GROUPS, E], BF16)
-        nc.sync.dma_start(out=w_rows[:], in_=W_qkv.rearrange("(a p) k -> p a k", p=P))
+        w_rows = []
+
+        def load_w(kind):
+            w_kind = const.tile([P, GROUPS, E], BF16, name="w_rows_%d" % kind)
+            nc.sync.dma_start(
+                out=w_kind[:],
+                in_=W_qkv.rearrange("(g a p) k -> a p g k", g=GROUPS, p=P)[kind],
+            )
+            w_rows.append(w_kind)
+
         x_words = {}
+
+        def load_x(b, first, size):
+            x_run = x_pool.tile([P, size * E], BF16, name="x_%d_%d" % (b, first))
+            nc.sync.dma_start(out=x_run[:], in_=x_rows[b][:, first * E : (first + size) * E])
+            for i in range(size):
+                x_words[(b, first + i)] = x_run[:].bitcast(F32)[:, i * WORDS : (i + 1) * WORDS]
+
+        load_w(0)
+        load_w(1)
         for b in range(B):
             first = 0
             for size in LOAD_SIZES[b]:
-                x_run = x_pool.tile([P, size * E], BF16, name="x_%d_%d" % (b, first))
-                nc.sync.dma_start(
-                    out=x_run[:], in_=x_rows[b][:, first * E : (first + size) * E]
-                )
-                for i in range(size):
-                    x_words[(b, first + i)] = x_run[:].bitcast(F32)[:, i * WORDS : (i + 1) * WORDS]
+                load_x(b, first, size)
+                if b == 0 and first == 0:
+                    load_w(2)
                 first += size
 
         warm_in = const.tile([P, 1], F32)
@@ -153,27 +161,27 @@ def tile_progenattention_pa_t_kernel(tc, hidden_states, W_qkv, out_0, out_1, out
         w_codes = const.tile([P, 3 * HD], U32, align_bytes=64)
         w_scales = const.tile([P, 3 * HD], U8, align_bytes=64)
         for kind in range(3):
-            w_t = psum.tile([P, 2, 2, P], F32, name="transposed")
+            w_t = psum.tile([P, 2, GROUPS, P], F32, name=("passing_ps", "v_ps", "rotated_ps")[kind])
             for g in range(GROUPS):
-                words = w_rows[:, 3 * g + kind, :].bitcast(F32)
+                words = w_rows[kind][:, g, :].bitcast(F32)
                 for u in range(2):
-                    nc.tensor.transpose(w_t[:, g, u, :], words[:, u:WORDS:2], identity[:])
+                    nc.tensor.transpose(w_t[:, u, g, :], words[:, u:WORDS:2], identity[:])
             if kind == 2:
                 nc.scalar.copy(
-                    out=w_words[:, 2 * HD : 3 * HD, :].rearrange("p (g r) u -> p g r u", g=GROUPS),
-                    in_=w_t[:].rearrange("p g u r -> p g r u"),
+                    out=w_words[:, 2 * HD : 3 * HD, :],
+                    in_=w_t[:].rearrange("p u g r -> p (g r) u"),
                 )
             else:
-                halves = w_t[:].rearrange("p g u (hh f d) -> p g f hh d u", hh=2, f=2)
+                halves = w_t[:].rearrange("p u g (hh f d) -> p f (g hh) d u", hh=2, f=2)
                 for f in range(2):
-                    for g in range(GROUPS):
-                        first = f * HD + kind * (HD // 2) + g * 2 * ROT
-                        nc.scalar.copy(
-                            out=w_words[:, first : first + 2 * ROT, :].rearrange(
-                                "p (hh d) u -> p hh d u", hh=2
-                            ),
-                            in_=halves[:, g, f, :, :, :],
-                        )
+                    first = f * HD + kind * (HD // 2)
+                    copy = (nc.vector.tensor_copy, nc.scalar.copy)[kind]
+                    copy(
+                        out=w_words[:, first : first + HD // 2, :].rearrange(
+                            "p (h d) u -> p h d u", h=H
+                        ),
+                        in_=halves[:, f, :, :, :],
+                    )
         for block in range(3):
             nc.vector.quantize_mx(
                 out=w_codes[:, block * HD : (block + 1) * HD].bitcast(FP8X4),
@@ -181,42 +189,71 @@ def tile_progenattention_pa_t_kernel(tc, hidden_states, W_qkv, out_0, out_1, out
                 in_=w_grouped[:, block * HD * 4 : (block + 1) * HD * 4],
             )
 
-        def transpose_pair(b, m):
-            transposed = psum.tile([P, 2, 2, P], F32, name="transposed")
-            for side in range(2):
-                words = x_words[(b, 2 * m + side)]
-                for u in range(2):
-                    nc.tensor.transpose(
-                        transposed[:, side, u, :], words[:, u:WORDS:2], identity[:]
-                    )
-            grouped = operand_pool.tile([P, 2 * E], BF16, align_bytes=64)
-            nc.scalar.copy(
-                out=grouped[:].bitcast(F32).rearrange("p (s r u) -> p s r u", s=2, u=2),
-                in_=transposed[:].rearrange("p s u r -> p s r u"),
-            )
+        def transpose_quad(quad):
+            grouped = operand_pool.tile([P, 4 * E], BF16, align_bytes=64)
+            for half, (b, m) in enumerate(quad):
+                transposed = psum.tile([P, 2, 2, P], F32, name="transposed")
+                for side in range(2):
+                    words = x_words[(b, 2 * m + side)]
+                    for u in range(2):
+                        nc.tensor.transpose(
+                            transposed[:, side, u, :], words[:, u:WORDS:2], identity[:]
+                        )
+                nc.scalar.copy(
+                    out=grouped[:, half * 2 * E : (half + 1) * 2 * E]
+                    .bitcast(F32)
+                    .rearrange("p (s r u) -> p s r u", s=2, u=2),
+                    in_=transposed[:].rearrange("p s u r -> p s r u"),
+                )
             return grouped
 
-        def quantise_pair(grouped):
-            codes = operand_pool.tile([P, 2 * P], U32, align_bytes=64)
-            scales = operand_pool.tile([P, 2 * P], U8, align_bytes=64)
-            nc.vector.quantize_mx(out=codes[:].bitcast(FP8X4), scales=scales[:], in_=grouped[:])
+        def quantise_quad(grouped, pieces):
+            codes = operand_pool.tile([P, 4 * P], U32, align_bytes=64)
+            scales = operand_pool.tile([P, 4 * P], U8, align_bytes=64)
+            width = 4 * P // pieces
+            for piece in range(pieces):
+                tokens = slice(piece * width, (piece + 1) * width)
+                nc.vector.quantize_mx(
+                    out=codes[:, tokens].bitcast(FP8X4),
+                    scales=scales[:, tokens],
+                    in_=grouped[:, piece * width * 4 : (piece + 1) * width * 4],
+                )
             return codes, scales
 
-        def project_pair(codes, scales, qk_stage, v_stage, m, t):
+        def project_pair(pair, half, codes, scales):
+            b, m = pair
+            first, size = store_run[pair]
+            if 2 * m == first:
+                qk_stage = stage_pool.tile([P, 2, MAX_STORE * HD], F32)
+                v_stage = stage_pool.tile([P, MAX_STORE * HD], F32)
+                stage_of[(b, first)] = (qk_stage, v_stage)
+            qk_stage, v_stage = stage_of[(b, first)]
+            columns = slice((2 * m - first) * HD, (2 * m - first + 2) * HD)
+            qk_out = qk_stage[:, :, columns].rearrange("p c (s h d) -> p c s h d", s=2, h=H)
+
             rotated_ps = psum.tile([P, 2 * HD], F32)
             passing_ps = psum.tile([P, 2 * HD], F32)
             v_ps = psum.tile([P, 2 * HD], F32)
             for block, bank in enumerate((rotated_ps, passing_ps, v_ps)):
                 for side in range(2):
+                    tokens = slice((2 * half + side) * P, (2 * half + side + 1) * P)
                     nc.tensor.matmul_mx(
                         out=bank[:, side * HD : (side + 1) * HD],
-                        lhsT=codes[:, side * P : (side + 1) * P].bitcast(FP8X4),
-                        lhsT_scale=scales[:, side * P : (side + 1) * P],
+                        lhsT=codes[:, tokens].bitcast(FP8X4),
+                        lhsT_scale=scales[:, tokens],
                         rhs=w_codes[:, block * HD : (block + 1) * HD].bitcast(FP8X4),
                         rhs_scale=w_scales[:, block * HD : (block + 1) * HD],
                         start=True,
                         stop=True,
                     )
+            nc.scalar.copy(
+                out=qk_out[:, :, :, :, ROT:DH],
+                in_=passing_ps[:].rearrange("p (s c h d) -> p c s h d", s=2, c=2, h=H),
+            )
+            nc.scalar.copy(out=v_stage[:, columns], in_=v_ps[:])
+            return rotated_ps, qk_out[:, :, :, :, 0:ROT]
+
+        def multiply_pair(pair, rotated_ps):
             products = operand_pool.tile([P, 2, 2 * HD], F32)
             shape = [P, 2, 2, 2 * H, ANGLES, 2]
             nc.vector.tensor_tensor(
@@ -225,62 +262,58 @@ def tile_progenattention_pa_t_kernel(tc, hidden_states, W_qkv, out_0, out_1, out
                 .rearrange("p (s c j k) -> p k s c j", s=2, c=2 * H, k=2)
                 .unsqueeze(5)
                 .to_broadcast(shape),
-                in1=tables[:, m, :, :, :]
+                in1=tables[:, pair[1], :, :, :]
                 .rearrange("p k s (j e) -> p k s j e", e=2)
                 .unsqueeze(3)
                 .to_broadcast(shape),
                 op=ALU.mult,
             )
-            nc.scalar.copy(
-                out=qk_stage[:, :, t * HD : (t + 2) * HD].rearrange(
-                    "p c (s h d) -> p c s h d", s=2, h=H
-                )[:, :, :, :, ROT:DH],
-                in_=passing_ps[:].rearrange("p (s c h d) -> p c s h d", s=2, c=2, h=H),
-            )
-            nc.scalar.copy(out=v_stage[:, t * HD : (t + 2) * HD], in_=v_ps[:])
             return products
 
-        def finish_pair(products, qk_stage, t):
+        def add_pair(engine, products, rotated_out):
             terms = products[:].rearrange("p k (s c h d) -> p k c s h d", s=2, c=2, h=H)
-            nc.vector.tensor_tensor(
-                out=qk_stage[:, :, t * HD : (t + 2) * HD].rearrange(
-                    "p c (s h d) -> p c s h d", s=2, h=H
-                )[:, :, :, :, 0:ROT],
+            engine.tensor_tensor(
+                out=rotated_out,
                 in0=terms[:, 0, :, :, :, :],
                 in1=terms[:, 1, :, :, :, :],
                 op=ALU.add,
             )
 
-        def store(b, first, size, qk_stage, v_stage):
-            columns = slice(first * HD, (first + size) * HD)
-            nc.sync.dma_start(out=out_rows[2][b][:, columns], in_=v_stage[:, 0 : size * HD])
-            nc.sync.dma_start(out=out_rows[0][b][:, columns], in_=qk_stage[:, 0, 0 : size * HD])
-            nc.sync.dma_start(out=out_rows[1][b][:, columns], in_=qk_stage[:, 1, 0 : size * HD])
-
-        grouped_of = {}
-        operand_of = {}
-        stage_of = {}
-        products_of = {}
-        for n in range(len(pairs) + 3):
-            if n < len(pairs):
-                grouped_of[n] = transpose_pair(*pairs[n])
-            if 0 <= n - 1 < len(pairs):
-                operand_of[n - 1] = quantise_pair(grouped_of[n - 1])
-            if 0 <= n - 2 < len(pairs):
-                b, m = pairs[n - 2]
-                first, size = store_run[(b, m)]
-                if 2 * m == first:
-                    qk_stage = stage_pool.tile([P, 2, MAX_STORE * HD], F32)
-                    v_stage = stage_pool.tile([P, MAX_STORE * HD], F32)
-                    stage_of[(b, first)] = (qk_stage, v_stage)
-                codes, scales = operand_of[n - 2]
-                products_of[n - 2] = project_pair(
-                    codes, scales, *stage_of[(b, first)], m, 2 * m - first
-                )
-            if 0 <= n - 3:
-                b, m = pairs[n - 3]
-                first, size = store_run[(b, m)]
+        def store_if_complete(pair):
+            b, m = pair
+            first, size = store_run[pair]
+            if 2 * m + 2 == first + size:
                 qk_stage, v_stage = stage_of[(b, first)]
-                finish_pair(products_of[n - 3], qk_stage, 2 * m - first)
-                if 2 * m + 2 == first + size:
-                    store(b, first, size, qk_stage, v_stage)
+                columns = slice(first * HD, (first + size) * HD)
+                nc.sync.dma_start(out=out_rows[2][b][:, columns], in_=v_stage[:, 0 : size * HD])
+                nc.sync.dma_start(out=out_rows[0][b][:, columns], in_=qk_stage[:, 0, 0 : size * HD])
+                nc.sync.dma_start(out=out_rows[1][b][:, columns], in_=qk_stage[:, 1, 0 : size * HD])
+
+        quads = [pairs[n : n + 2] for n in range(0, len(pairs), 2)]
+        last_round = len(quads) - 1
+        stage_of = {}
+        grouped_of = {}
+        projected = {}
+        with tc.manual_schedule():
+            for r in range(-2, len(quads)):
+                rotating, quantising, transposing = 0 <= r, 0 <= r + 1 <= last_round, r + 2 <= last_round
+                if rotating:
+                    first_pair, second_pair = quads[r]
+                    (first_ps, first_out), (second_ps, second_out) = projected[r]
+                    first_products = multiply_pair(first_pair, first_ps)
+                if quantising:
+                    codes, scales = quantise_quad(grouped_of[r + 1], 2 if r + 1 == 0 else 1)
+                if rotating:
+                    add_pair(nc.vector, first_products, first_out)
+                    store_if_complete(first_pair)
+                if quantising:
+                    projected[r + 1] = [project_pair(quads[r + 1][0], 0, codes, scales)]
+                if transposing:
+                    grouped_of[r + 2] = transpose_quad(quads[r + 2])
+                if rotating:
+                    second_products = multiply_pair(second_pair, second_ps)
+                    engine = nc.vector if r == last_round else nc.gpsimd
+                    add_pair(engine, second_products, second_out)
+                    store_if_complete(second_pair)
+                if quantising:
+                    projected[r + 1].append(project_pair(quads[r + 1][1], 1, codes, scales))

@@ -21,7 +21,7 @@ ANGLES = ROT // 2
 POS_PER_PART = S // P
 WORDS = E // 2
 PAIRS = POS_PER_PART // 2
-LOAD_SIZES = [[2, 6, 8], [16], [16], [16]]
+LOAD_SIZES = [[2, 2, 4, 8], [16], [16], [16]]
 STORE_SIZES = [[8, 8], [8, 8], [8, 8], [8, 4, 2, 2]]
 MAX_STORE = max(max(sizes) for sizes in STORE_SIZES)
 ROUND_MAGIC = 12582912.0
@@ -220,7 +220,22 @@ def tile_progenattention_pa_t_kernel(tc, hidden_states, W_qkv, out_0, out_1, out
                 )
             return codes, scales
 
-        def project_pair(pair, half, codes, scales):
+        def multiply_weights(block, half, codes, scales):
+            bank = psum.tile([P, 2 * HD], F32, name=("rotated_ps", "passing_ps", "v_ps")[block])
+            for side in range(2):
+                tokens = slice((2 * half + side) * P, (2 * half + side + 1) * P)
+                nc.tensor.matmul_mx(
+                    out=bank[:, side * HD : (side + 1) * HD],
+                    lhsT=codes[:, tokens].bitcast(FP8X4),
+                    lhsT_scale=scales[:, tokens],
+                    rhs=w_codes[:, block * HD : (block + 1) * HD].bitcast(FP8X4),
+                    rhs_scale=w_scales[:, block * HD : (block + 1) * HD],
+                    start=True,
+                    stop=True,
+                )
+            return bank
+
+        def pass_pair(pair, half, codes, scales):
             b, m = pair
             first, size = store_run[pair]
             if 2 * m == first:
@@ -231,27 +246,14 @@ def tile_progenattention_pa_t_kernel(tc, hidden_states, W_qkv, out_0, out_1, out
             columns = slice((2 * m - first) * HD, (2 * m - first + 2) * HD)
             qk_out = qk_stage[:, :, columns].rearrange("p c (s h d) -> p c s h d", s=2, h=H)
 
-            rotated_ps = psum.tile([P, 2 * HD], F32)
-            passing_ps = psum.tile([P, 2 * HD], F32)
-            v_ps = psum.tile([P, 2 * HD], F32)
-            for block, bank in enumerate((rotated_ps, passing_ps, v_ps)):
-                for side in range(2):
-                    tokens = slice((2 * half + side) * P, (2 * half + side + 1) * P)
-                    nc.tensor.matmul_mx(
-                        out=bank[:, side * HD : (side + 1) * HD],
-                        lhsT=codes[:, tokens].bitcast(FP8X4),
-                        lhsT_scale=scales[:, tokens],
-                        rhs=w_codes[:, block * HD : (block + 1) * HD].bitcast(FP8X4),
-                        rhs_scale=w_scales[:, block * HD : (block + 1) * HD],
-                        start=True,
-                        stop=True,
-                    )
+            passing_ps = multiply_weights(1, half, codes, scales)
+            v_ps = multiply_weights(2, half, codes, scales)
             nc.scalar.copy(
                 out=qk_out[:, :, :, :, ROT:DH],
                 in_=passing_ps[:].rearrange("p (s c h d) -> p c s h d", s=2, c=2, h=H),
             )
             nc.scalar.copy(out=v_stage[:, columns], in_=v_ps[:])
-            return rotated_ps, qk_out[:, :, :, :, 0:ROT]
+            return qk_out[:, :, :, :, 0:ROT]
 
         def multiply_pair(pair, rotated_ps):
             products = operand_pool.tile([P, 2, 2 * HD], F32)
@@ -293,27 +295,31 @@ def tile_progenattention_pa_t_kernel(tc, hidden_states, W_qkv, out_0, out_1, out
         last_round = len(quads) - 1
         stage_of = {}
         grouped_of = {}
-        projected = {}
+        rotated_of = {}
         with tc.manual_schedule():
             for r in range(-2, len(quads)):
                 rotating, quantising, transposing = 0 <= r, 0 <= r + 1 <= last_round, r + 2 <= last_round
                 if rotating:
-                    first_pair, second_pair = quads[r]
-                    (first_ps, first_out), (second_ps, second_out) = projected[r]
-                    first_products = multiply_pair(first_pair, first_ps)
+                    pair_a, pair_b = quads[r]
+                    products_a = multiply_pair(pair_a, rotated_of[pair_a][0])
+                if transposing and rotating:
+                    grouped_of[r + 2] = transpose_quad(quads[r + 2])
                 if quantising:
                     codes, scales = quantise_quad(grouped_of[r + 1], 2 if r + 1 == 0 else 1)
                 if rotating:
-                    add_pair(nc.vector, first_products, first_out)
-                    store_if_complete(first_pair)
+                    add_pair(nc.vector, products_a, rotated_of[pair_a][1])
+                    store_if_complete(pair_a)
                 if quantising:
-                    projected[r + 1] = [project_pair(quads[r + 1][0], 0, codes, scales)]
-                if transposing:
-                    grouped_of[r + 2] = transpose_quad(quads[r + 2])
+                    next_a, next_b = quads[r + 1]
+                    rotated_ps = multiply_weights(0, 0, codes, scales)
+                    rotated_of[next_a] = (rotated_ps, pass_pair(next_a, 0, codes, scales))
+                    rotated_out = pass_pair(next_b, 1, codes, scales)
                 if rotating:
-                    second_products = multiply_pair(second_pair, second_ps)
+                    products_b = multiply_pair(pair_b, rotated_of[pair_b][0])
                     engine = nc.vector if r == last_round else nc.gpsimd
-                    add_pair(engine, second_products, second_out)
-                    store_if_complete(second_pair)
+                    add_pair(engine, products_b, rotated_of[pair_b][1])
+                    store_if_complete(pair_b)
                 if quantising:
-                    projected[r + 1].append(project_pair(quads[r + 1][1], 1, codes, scales))
+                    rotated_of[next_b] = (multiply_weights(0, 1, codes, scales), rotated_out)
+                if transposing and not rotating:
+                    grouped_of[r + 2] = transpose_quad(quads[r + 2])

@@ -255,31 +255,35 @@ def tile_progenattention_pa_t_kernel(tc, hidden_states, W_qkv, out_0, out_1, out
             nc.scalar.copy(out=v_stage[:, columns], in_=v_ps[:])
             return qk_out[:, :, :, :, 0:ROT]
 
-        def multiply_pair(pair, rotated_ps):
+        def multiply_pair(pair, rotated_ps, parts):
             products = operand_pool.tile([P, 2, 2 * HD], F32)
-            shape = [P, 2, 2, 2 * H, ANGLES, 2]
-            nc.vector.tensor_tensor(
-                out=products[:].rearrange("p k (s c j e) -> p k s c j e", s=2, c=2 * H, e=2),
-                in0=rotated_ps[:]
-                .rearrange("p (s c j k) -> p k s c j", s=2, c=2 * H, k=2)
-                .unsqueeze(5)
-                .to_broadcast(shape),
-                in1=tables[:, pair[1], :, :, :]
-                .rearrange("p k s (j e) -> p k s j e", e=2)
-                .unsqueeze(3)
-                .to_broadcast(shape),
-                op=ALU.mult,
-            )
+            for sides in parts:
+                shape = [P, 2, sides.stop - sides.start, 2 * H, ANGLES, 2]
+                nc.vector.tensor_tensor(
+                    out=products[:].rearrange("p k (s c j e) -> p k s c j e", s=2, c=2 * H, e=2)[
+                        :, :, sides, :, :, :
+                    ],
+                    in0=rotated_ps[:]
+                    .rearrange("p (s c j k) -> p k s c j", s=2, c=2 * H, k=2)[:, :, sides, :, :]
+                    .unsqueeze(5)
+                    .to_broadcast(shape),
+                    in1=tables[:, pair[1], :, sides, :]
+                    .rearrange("p k s (j e) -> p k s j e", e=2)
+                    .unsqueeze(3)
+                    .to_broadcast(shape),
+                    op=ALU.mult,
+                )
             return products
 
-        def add_pair(engine, products, rotated_out):
+        def add_pair(engine, products, rotated_out, parts):
             terms = products[:].rearrange("p k (s c h d) -> p k c s h d", s=2, c=2, h=H)
-            engine.tensor_tensor(
-                out=rotated_out,
-                in0=terms[:, 0, :, :, :, :],
-                in1=terms[:, 1, :, :, :, :],
-                op=ALU.add,
-            )
+            for sides in parts:
+                engine.tensor_tensor(
+                    out=rotated_out[:, :, sides, :, :],
+                    in0=terms[:, 0, :, sides, :, :],
+                    in1=terms[:, 1, :, sides, :, :],
+                    op=ALU.add,
+                )
 
         def store_if_complete(pair):
             b, m = pair
@@ -293,6 +297,8 @@ def tile_progenattention_pa_t_kernel(tc, hidden_states, W_qkv, out_0, out_1, out
 
         quads = [pairs[n : n + 2] for n in range(0, len(pairs), 2)]
         last_round = len(quads) - 1
+        whole = [slice(0, 2)]
+        halves = [slice(0, 1), slice(1, 2)]
         stage_of = {}
         grouped_of = {}
         rotated_of = {}
@@ -301,13 +307,13 @@ def tile_progenattention_pa_t_kernel(tc, hidden_states, W_qkv, out_0, out_1, out
                 rotating, quantising, transposing = 0 <= r, 0 <= r + 1 <= last_round, r + 2 <= last_round
                 if rotating:
                     pair_a, pair_b = quads[r]
-                    products_a = multiply_pair(pair_a, rotated_of[pair_a][0])
+                    products_a = multiply_pair(pair_a, rotated_of[pair_a][0], whole)
                 if transposing and rotating:
                     grouped_of[r + 2] = transpose_quad(quads[r + 2])
                 if quantising:
                     codes, scales = quantise_quad(grouped_of[r + 1], 2 if r + 1 == 0 else 1)
                 if rotating:
-                    add_pair(nc.vector, products_a, rotated_of[pair_a][1])
+                    add_pair(nc.vector, products_a, rotated_of[pair_a][1], whole)
                     store_if_complete(pair_a)
                 if quantising:
                     next_a, next_b = quads[r + 1]
@@ -315,9 +321,9 @@ def tile_progenattention_pa_t_kernel(tc, hidden_states, W_qkv, out_0, out_1, out
                     rotated_of[next_a] = (rotated_ps, pass_pair(next_a, 0, codes, scales))
                     rotated_out = pass_pair(next_b, 1, codes, scales)
                 if rotating:
-                    products_b = multiply_pair(pair_b, rotated_of[pair_b][0])
+                    products_b = multiply_pair(pair_b, rotated_of[pair_b][0], halves)
                     engine = nc.vector if r == last_round else nc.gpsimd
-                    add_pair(engine, products_b, rotated_of[pair_b][1])
+                    add_pair(engine, products_b, rotated_of[pair_b][1], halves)
                     store_if_complete(pair_b)
                 if quantising:
                     rotated_of[next_b] = (multiply_weights(0, 1, codes, scales), rotated_out)

@@ -29,7 +29,7 @@ ROUND_MAGIC = 12582912.0
 FLOPS = 2 * B * S * E * 3 * HD
 
 
-def build_rope_tables(nc, pool, tables):
+def start_rope_tables(nc, pool):
     turns_per_position = [
         1.0 / (2.0 * math.pi * 10000.0 ** (2.0 * j / ROT)) for j in range(ANGLES)
     ]
@@ -44,7 +44,6 @@ def build_rope_tables(nc, pool, tables):
         channel_multiplier=POS_PER_PART,
         allow_small_or_imprecise_dtypes=True,
     )
-
     coarse = pool.tile([P, POS_PER_PART, ANGLES], F32)
     fine = pool.tile([P, POS_PER_PART, ANGLES], F32)
     for j in range(ANGLES):
@@ -52,41 +51,64 @@ def build_rope_tables(nc, pool, tables):
             out=coarse[:, :, j], in0=position[:], scalar1=g_hi[j], scalar2=None, op0=ALU.mult
         )
         nc.scalar.activation(out=fine[:, :, j], in_=position[:], func=ACT.Copy, scale=g_lo[j])
-    nearest = pool.tile([P, POS_PER_PART, ANGLES], F32)
+    nearest = pool.tile([P, POS_PER_PART, ANGLES], F32, name="nearest_coarse")
+    nearest_integer(nc, coarse[:], nearest[:])
+    nc.vector.tensor_tensor(out=coarse[:], in0=coarse[:], in1=nearest[:], op=ALU.subtract)
+    return coarse, fine
 
-    def to_nearest_integer(values):
-        nc.vector.tensor_scalar(
-            out=nearest[:],
-            in0=values[:],
-            scalar1=ROUND_MAGIC,
-            scalar2=ROUND_MAGIC,
-            op0=ALU.add,
-            op1=ALU.subtract,
-        )
-        nc.vector.tensor_tensor(out=values[:], in0=values[:], in1=nearest[:], op=ALU.subtract)
 
-    to_nearest_integer(coarse)
-    turns = pool.tile([P, POS_PER_PART, ANGLES], F32)
-    nc.vector.tensor_tensor(out=turns[:], in0=coarse[:], in1=fine[:], op=ALU.add)
-    to_nearest_integer(turns)
-
-    above = pool.tile([P, POS_PER_PART, ANGLES], F32)
+def nearest_integer(nc, values, nearest):
     nc.vector.tensor_scalar(
-        out=above[:], in0=turns[:], scalar1=0.25, scalar2=None, op0=ALU.is_gt
+        out=nearest,
+        in0=values,
+        scalar1=ROUND_MAGIC,
+        scalar2=ROUND_MAGIC,
+        op0=ALU.add,
+        op1=ALU.subtract,
     )
-    argument = pool.tile([P, PAIRS, 2, 2, ANGLES, 2], F32)
-    paired = turns[:].rearrange("p (m s) j -> p m s j", s=2)
-    shifted = pool.tile([P, POS_PER_PART, ANGLES], F32)
-    nc.vector.scalar_tensor_tensor(
-        out=shifted[:], in0=turns[:], scalar=0.25, in1=above[:], op0=ALU.add, op1=ALU.subtract
-    )
-    paired_shifted = shifted[:].rearrange("p (m s) j -> p m s j", s=2)
-    nc.vector.tensor_copy(out=argument[:, :, 0, :, :, 0], in_=paired_shifted)
-    nc.vector.tensor_copy(out=argument[:, :, 0, :, :, 1], in_=paired)
-    nc.vector.tensor_scalar_mul(out=argument[:, :, 1, :, :, 0], in0=paired, scalar1=-1.0)
-    nc.vector.tensor_copy(out=argument[:, :, 1, :, :, 1], in_=paired_shifted)
+
+
+def rope_arguments(nc, pool, coarse, fine, parts):
+    work = []
+    for first, last in parts:
+        positions = slice(2 * first, 2 * last)
+        turns, nearest, shifted = [
+            pool.tile([P, 2 * (last - first), ANGLES], F32, name="%s_%d" % (what, first))
+            for what in ("turns", "nearest", "shifted")
+        ]
+        argument = pool.tile([P, last - first, 2, 2, ANGLES, 2], F32, name="argument_%d" % first)
+        work.append((turns, nearest, shifted, argument, positions))
+
+    for turns, nearest, shifted, argument, positions in work:
+        nc.vector.tensor_tensor(
+            out=turns[:], in0=coarse[:, positions, :], in1=fine[:, positions, :], op=ALU.add
+        )
+    for turns, nearest, shifted, argument, positions in work:
+        nearest_integer(nc, turns[:], nearest[:])
+    for turns, nearest, shifted, argument, positions in work:
+        nc.vector.tensor_tensor(out=turns[:], in0=turns[:], in1=nearest[:], op=ALU.subtract)
+    for turns, nearest, shifted, argument, positions in work:
+        nc.vector.tensor_scalar(
+            out=nearest[:], in0=turns[:], scalar1=0.25, scalar2=None, op0=ALU.is_gt
+        )
+    for turns, nearest, shifted, argument, positions in work:
+        nc.vector.scalar_tensor_tensor(
+            out=shifted[:], in0=turns[:], scalar=0.25, in1=nearest[:], op0=ALU.add, op1=ALU.subtract
+        )
+    for turns, nearest, shifted, argument, positions in work:
+        sin_turns, cos_turns = [
+            values[:].rearrange("p (m s) j -> p m s j", s=2) for values in (turns, shifted)
+        ]
+        nc.vector.tensor_copy(out=argument[:, :, 0, :, :, 1], in_=sin_turns)
+        nc.vector.tensor_scalar_mul(out=argument[:, :, 1, :, :, 0], in0=sin_turns, scalar1=-1.0)
+        nc.vector.tensor_copy(out=argument[:, :, 0, :, :, 0], in_=cos_turns)
+        nc.vector.tensor_copy(out=argument[:, :, 1, :, :, 1], in_=cos_turns)
+    return [argument for turns, nearest, shifted, argument, positions in work]
+
+
+def finish_rope_tables(nc, tables, argument, first, last):
     nc.scalar.activation(
-        out=tables[:].rearrange("p m k s c -> p (m k s c)"),
+        out=tables[:, first:last, :, :, :].rearrange("p m k s c -> p (m k s c)"),
         in_=argument[:].rearrange("p m k s j e -> p (m k s j e)"),
         func=ACT.Sin,
         scale=2.0 * math.pi,
@@ -101,6 +123,7 @@ def tile_progenattention_pa_t_kernel(tc, hidden_states, W_qkv, out_0, out_1, out
         operand_pool = ctx.enter_context(tc.tile_pool(name="operand_pool", bufs=3))
         stage_pool = ctx.enter_context(tc.tile_pool(name="stage_pool", bufs=4))
         psum = ctx.enter_context(tc.psum_pool(name="psum", bufs=2))
+        ctx.enter_context(tc.manual_schedule())
 
         x_rows = [hidden_states[b].rearrange("(p i) k -> p (i k)", i=POS_PER_PART) for b in range(B)]
         out_rows = [
@@ -145,79 +168,67 @@ def tile_progenattention_pa_t_kernel(tc, hidden_states, W_qkv, out_0, out_1, out
                     load_w(2)
                 first += size
 
-        warm_in = const.tile([P, 1], F32)
-        warm_out = const.tile([P, 1], F32)
-        nc.vector.memset(warm_in[:], 0.0)
-        nc.scalar.activation(out=warm_out[:], in_=warm_in[:], func=ACT.Sin)
-
-        tables = const.tile([P, PAIRS, 2, 2, ROT], F32)
-        build_rope_tables(nc, const, tables)
-
-        identity = const.tile([P, P], F32)
-        make_identity(nc, identity[:])
-
         w_grouped = const.tile([P, 3 * HD * 4], BF16, align_bytes=64)
         w_words = w_grouped[:].bitcast(F32).rearrange("p (c u) -> p c u", u=2)
         w_codes = const.tile([P, 3 * HD], U32, align_bytes=64)
         w_scales = const.tile([P, 3 * HD], U8, align_bytes=64)
-        for kind in range(3):
-            w_t = psum.tile([P, 2, GROUPS, P], F32, name=("passing_ps", "v_ps", "rotated_ps")[kind])
+
+        def transpose_w(kind, tag):
+            w_t = psum.tile([P, 2, GROUPS, P], F32, name=tag)
             for g in range(GROUPS):
                 words = w_rows[kind][:, g, :].bitcast(F32)
                 for u in range(2):
                     nc.tensor.transpose(w_t[:, u, g, :], words[:, u:WORDS:2], identity[:])
-            if kind == 2:
+            return w_t
+
+        def sort_w(kind, w_t):
+            halves = w_t[:].rearrange("p u g (hh f d) -> p f (g hh) d u", hh=2, f=2)
+            for f in range(2):
+                first = f * HD + kind * (HD // 2)
                 nc.scalar.copy(
-                    out=w_words[:, 2 * HD : 3 * HD, :],
-                    in_=w_t[:].rearrange("p u g r -> p (g r) u"),
+                    out=w_words[:, first : first + HD // 2, :].rearrange("p (h d) u -> p h d u", h=H),
+                    in_=halves[:, f, :, :, :],
                 )
-            else:
-                halves = w_t[:].rearrange("p u g (hh f d) -> p f (g hh) d u", hh=2, f=2)
-                for f in range(2):
-                    first = f * HD + kind * (HD // 2)
-                    copy = (nc.vector.tensor_copy, nc.scalar.copy)[kind]
-                    copy(
-                        out=w_words[:, first : first + HD // 2, :].rearrange(
-                            "p (h d) u -> p h d u", h=H
-                        ),
-                        in_=halves[:, f, :, :, :],
-                    )
-        for block in range(3):
+
+        def quantise_w(block):
+            columns = slice(block * HD, (block + 1) * HD)
             nc.vector.quantize_mx(
-                out=w_codes[:, block * HD : (block + 1) * HD].bitcast(FP8X4),
-                scales=w_scales[:, block * HD : (block + 1) * HD],
+                out=w_codes[:, columns].bitcast(FP8X4),
+                scales=w_scales[:, columns],
                 in_=w_grouped[:, block * HD * 4 : (block + 1) * HD * 4],
             )
 
-        def transpose_quad(quad):
-            grouped = operand_pool.tile([P, 4 * E], BF16, align_bytes=64)
-            for half, (b, m) in enumerate(quad):
-                transposed = psum.tile([P, 2, 2, P], F32, name="transposed")
-                for side in range(2):
-                    words = x_words[(b, 2 * m + side)]
-                    for u in range(2):
-                        nc.tensor.transpose(
-                            transposed[:, side, u, :], words[:, u:WORDS:2], identity[:]
-                        )
-                nc.scalar.copy(
-                    out=grouped[:, half * 2 * E : (half + 1) * 2 * E]
-                    .bitcast(F32)
-                    .rearrange("p (s r u) -> p s r u", s=2, u=2),
-                    in_=transposed[:].rearrange("p s u r -> p s r u"),
-                )
-            return grouped
+        stage_of = {}
 
-        def quantise_quad(grouped, pieces):
+        def transpose_pair(pair, half, grouped):
+            b, m = pair
+            transposed = psum.tile([P, 2, 2, P], F32, name="transposed")
+            for side in range(2):
+                words = x_words[(b, 2 * m + side)]
+                for u in range(2):
+                    nc.tensor.transpose(
+                        transposed[:, side, u, :], words[:, u:WORDS:2], identity[:]
+                    )
+            nc.scalar.copy(
+                out=grouped[:, half * 2 * E : (half + 1) * 2 * E]
+                .bitcast(F32)
+                .rearrange("p (s r u) -> p s r u", s=2, u=2),
+                in_=transposed[:].rearrange("p s u r -> p s r u"),
+            )
+
+        def quantise_tokens(grouped, codes, scales, first, last):
+            nc.vector.quantize_mx(
+                out=codes[:, first * P : last * P].bitcast(FP8X4),
+                scales=scales[:, first * P : last * P],
+                in_=grouped[:, first * E : last * E],
+            )
+
+        def new_grouped():
+            return operand_pool.tile([P, 4 * E], BF16, align_bytes=64, name="grouped")
+
+        def new_operand():
             codes = operand_pool.tile([P, 4 * P], U32, align_bytes=64)
             scales = operand_pool.tile([P, 4 * P], U8, align_bytes=64)
-            width = 4 * P // pieces
-            for piece in range(pieces):
-                tokens = slice(piece * width, (piece + 1) * width)
-                nc.vector.quantize_mx(
-                    out=codes[:, tokens].bitcast(FP8X4),
-                    scales=scales[:, tokens],
-                    in_=grouped[:, piece * width * 4 : (piece + 1) * width * 4],
-                )
             return codes, scales
 
         def multiply_weights(block, half, codes, scales):
@@ -295,37 +306,66 @@ def tile_progenattention_pa_t_kernel(tc, hidden_states, W_qkv, out_0, out_1, out
                 nc.sync.dma_start(out=out_rows[0][b][:, columns], in_=qk_stage[:, 0, 0 : size * HD])
                 nc.sync.dma_start(out=out_rows[1][b][:, columns], in_=qk_stage[:, 1, 0 : size * HD])
 
+        warm_in = const.tile([P, 1], F32)
+        warm_out = const.tile([P, 1], F32)
+        nc.vector.memset(warm_in[:], 0.0)
+        nc.scalar.activation(out=warm_out[:], in_=warm_in[:], func=ACT.Sin)
+        tables = const.tile([P, PAIRS, 2, 2, ROT], F32)
+        coarse, fine = start_rope_tables(nc, const)
+        identity = const.tile([P, P], F32)
+        make_identity(nc, identity[:])
+
         quads = [pairs[n : n + 2] for n in range(0, len(pairs), 2)]
         last_round = len(quads) - 1
         whole = [slice(0, 2)]
         halves = [slice(0, 1), slice(1, 2)]
-        stage_of = {}
-        grouped_of = {}
+        grouped_of = {0: new_grouped(), 1: new_grouped()}
         rotated_of = {}
-        with tc.manual_schedule():
-            for r in range(-2, len(quads)):
-                rotating, quantising, transposing = 0 <= r, 0 <= r + 1 <= last_round, r + 2 <= last_round
-                if rotating:
-                    pair_a, pair_b = quads[r]
-                    products_a = multiply_pair(pair_a, rotated_of[pair_a][0], whole)
-                if transposing and rotating:
-                    grouped_of[r + 2] = transpose_quad(quads[r + 2])
-                if quantising:
-                    codes, scales = quantise_quad(grouped_of[r + 1], 2 if r + 1 == 0 else 1)
-                if rotating:
-                    add_pair(nc.vector, products_a, rotated_of[pair_a][1], whole)
-                    store_if_complete(pair_a)
-                if quantising:
-                    next_a, next_b = quads[r + 1]
-                    rotated_ps = multiply_weights(0, 0, codes, scales)
-                    rotated_of[next_a] = (rotated_ps, pass_pair(next_a, 0, codes, scales))
-                    rotated_out = pass_pair(next_b, 1, codes, scales)
-                if rotating:
-                    products_b = multiply_pair(pair_b, rotated_of[pair_b][0], halves)
-                    engine = nc.vector if r == last_round else nc.gpsimd
-                    add_pair(engine, products_b, rotated_of[pair_b][1], halves)
-                    store_if_complete(pair_b)
-                if quantising:
-                    rotated_of[next_b] = (multiply_weights(0, 1, codes, scales), rotated_out)
-                if transposing and not rotating:
-                    grouped_of[r + 2] = transpose_quad(quads[r + 2])
+
+        for kind, tag in ((0, "passing_ps"), (1, "v_ps")):
+            sort_w(kind, transpose_w(kind, tag))
+        transpose_pair(quads[0][0], 0, grouped_of[0])
+        early, late = rope_arguments(nc, const, coarse, fine, ((0, 2), (2, PAIRS)))
+        finish_rope_tables(nc, tables, early, 0, 2)
+        w_v = transpose_w(2, "rotated_ps")
+        transpose_pair(quads[0][1], 1, grouped_of[0])
+        nc.scalar.copy(
+            out=w_words[:, 2 * HD : 3 * HD, :], in_=w_v[:].rearrange("p u g r -> p (g r) u")
+        )
+        for half in range(2):
+            transpose_pair(quads[1][half], half, grouped_of[1])
+        codes, scales = new_operand()
+        quantise_w(0)
+        quantise_tokens(grouped_of[0], codes, scales, 0, 2)
+        rotated_a = multiply_weights(0, 0, codes, scales)
+        quantise_w(1)
+        quantise_tokens(grouped_of[0], codes, scales, 2, 4)
+        quantise_w(2)
+        rotated_of[quads[0][0]] = (rotated_a, pass_pair(quads[0][0], 0, codes, scales))
+        rotated_out = pass_pair(quads[0][1], 1, codes, scales)
+        rotated_of[quads[0][1]] = (multiply_weights(0, 1, codes, scales), rotated_out)
+        finish_rope_tables(nc, tables, late, 2, PAIRS)
+
+        for r in range(len(quads)):
+            pair_a, pair_b = quads[r]
+            products_a = multiply_pair(pair_a, rotated_of[pair_a][0], whole)
+            if r + 2 <= last_round:
+                grouped_of[r + 2] = new_grouped()
+                for half in range(2):
+                    transpose_pair(quads[r + 2][half], half, grouped_of[r + 2])
+            if r + 1 <= last_round:
+                codes, scales = new_operand()
+                quantise_tokens(grouped_of[r + 1], codes, scales, 0, 4)
+            add_pair(nc.vector, products_a, rotated_of[pair_a][1], whole)
+            store_if_complete(pair_a)
+            if r + 1 <= last_round:
+                next_a, next_b = quads[r + 1]
+                rotated_a = multiply_weights(0, 0, codes, scales)
+                rotated_of[next_a] = (rotated_a, pass_pair(next_a, 0, codes, scales))
+                rotated_out = pass_pair(next_b, 1, codes, scales)
+            products_b = multiply_pair(pair_b, rotated_of[pair_b][0], halves)
+            engine = nc.vector if r == last_round else nc.gpsimd
+            add_pair(engine, products_b, rotated_of[pair_b][1], halves)
+            store_if_complete(pair_b)
+            if r + 1 <= last_round:
+                rotated_of[next_b] = (multiply_weights(0, 1, codes, scales), rotated_out)

import math
from contextlib import ExitStack

import concourse.mybir as mybir
from concourse.masks import make_identity

F32 = mybir.dt.float32
BF16 = mybir.dt.bfloat16
U32 = mybir.dt.uint32
U8 = mybir.dt.uint8
FP8X4 = mybir.dt.float8_e4m3fn_x4
ALU = mybir.AluOpType
ACT = mybir.ActivationFunctionType

P = 128
B, S, E = 4, 2048, 512
H, DH, ROT = 4, 64, 32
HD = H * DH
GROUPS = 2
ANGLES = ROT // 2
POS_PER_PART = S // P
WORDS = E // 2
PAIRS = POS_PER_PART // 2
LOAD_SIZES = [[2, 2, 4, 8], [16], [16], [16]]
STORE_SIZES = [[8, 8], [8, 8], [8, 8], [8, 4, 2, 2]]
MAX_STORE = max(max(sizes) for sizes in STORE_SIZES)
ROUND_MAGIC = 12582912.0

FLOPS = 2 * B * S * E * 3 * HD


def start_rope_tables(nc, pool):
    turns_per_position = [
        1.0 / (2.0 * math.pi * 10000.0 ** (2.0 * j / ROT)) for j in range(ANGLES)
    ]
    g_hi = [round(g * 32768.0) / 32768.0 for g in turns_per_position]
    g_lo = [g - hi for g, hi in zip(turns_per_position, g_hi)]

    position = pool.tile([P, POS_PER_PART], F32)
    nc.gpsimd.iota(
        position[:],
        pattern=[[1, POS_PER_PART]],
        base=0,
        channel_multiplier=POS_PER_PART,
        allow_small_or_imprecise_dtypes=True,
    )
    coarse = pool.tile([P, POS_PER_PART, ANGLES], F32)
    fine = pool.tile([P, POS_PER_PART, ANGLES], F32)
    for j in range(ANGLES):
        nc.vector.tensor_scalar(
            out=coarse[:, :, j], in0=position[:], scalar1=g_hi[j], scalar2=None, op0=ALU.mult
        )
        nc.scalar.activation(out=fine[:, :, j], in_=position[:], func=ACT.Copy, scale=g_lo[j])
    nearest = pool.tile([P, POS_PER_PART, ANGLES], F32, name="nearest_coarse")
    nearest_integer(nc, coarse[:], nearest[:])
    nc.vector.tensor_tensor(out=coarse[:], in0=coarse[:], in1=nearest[:], op=ALU.subtract)
    return coarse, fine


def nearest_integer(nc, values, nearest):
    nc.vector.tensor_scalar(
        out=nearest,
        in0=values,
        scalar1=ROUND_MAGIC,
        scalar2=ROUND_MAGIC,
        op0=ALU.add,
        op1=ALU.subtract,
    )


def rope_arguments(nc, pool, coarse, fine, parts):
    work = []
    for first, last in parts:
        positions = slice(2 * first, 2 * last)
        turns, nearest, shifted = [
            pool.tile([P, 2 * (last - first), ANGLES], F32, name="%s_%d" % (what, first))
            for what in ("turns", "nearest", "shifted")
        ]
        argument = pool.tile([P, last - first, 2, 2, ANGLES, 2], F32, name="argument_%d" % first)
        work.append((turns, nearest, shifted, argument, positions))

    for turns, nearest, shifted, argument, positions in work:
        nc.vector.tensor_tensor(
            out=turns[:], in0=coarse[:, positions, :], in1=fine[:, positions, :], op=ALU.add
        )
    for turns, nearest, shifted, argument, positions in work:
        nearest_integer(nc, turns[:], nearest[:])
    for turns, nearest, shifted, argument, positions in work:
        nc.vector.tensor_tensor(out=turns[:], in0=turns[:], in1=nearest[:], op=ALU.subtract)
    for turns, nearest, shifted, argument, positions in work:
        nc.vector.tensor_scalar(
            out=nearest[:], in0=turns[:], scalar1=0.25, scalar2=None, op0=ALU.is_gt
        )
    for turns, nearest, shifted, argument, positions in work:
        nc.vector.scalar_tensor_tensor(
            out=shifted[:], in0=turns[:], scalar=0.25, in1=nearest[:], op0=ALU.add, op1=ALU.subtract
        )
    for turns, nearest, shifted, argument, positions in work:
        sin_turns, cos_turns = [
            values[:].rearrange("p (m s) j -> p m s j", s=2) for values in (turns, shifted)
        ]
        nc.vector.tensor_copy(out=argument[:, :, 0, :, :, 1], in_=sin_turns)
        nc.vector.tensor_scalar_mul(out=argument[:, :, 1, :, :, 0], in0=sin_turns, scalar1=-1.0)
        nc.vector.tensor_copy(out=argument[:, :, 0, :, :, 0], in_=cos_turns)
        nc.vector.tensor_copy(out=argument[:, :, 1, :, :, 1], in_=cos_turns)
    return [argument for turns, nearest, shifted, argument, positions in work]


def finish_rope_tables(nc, tables, argument, first, last):
    nc.scalar.activation(
        out=tables[:, first:last, :, :, :].rearrange("p m k s c -> p (m k s c)"),
        in_=argument[:].rearrange("p m k s j e -> p (m k s j e)"),
        func=ACT.Sin,
        scale=2.0 * math.pi,
    )


def tile_progenattention_pa_t_kernel(tc, hidden_states, W_qkv, out_0, out_1, out_2):
    nc = tc.nc
    with ExitStack() as ctx:
        const = ctx.enter_context(tc.tile_pool(name="const", bufs=1))
        x_pool = ctx.enter_context(tc.tile_pool(name="x_pool", bufs=1))
        operand_pool = ctx.enter_context(tc.tile_pool(name="operand_pool", bufs=3))
        stage_pool = ctx.enter_context(tc.tile_pool(name="stage_pool", bufs=4))
        psum = ctx.enter_context(tc.psum_pool(name="psum", bufs=2))
        ctx.enter_context(tc.manual_schedule())

        x_rows = [hidden_states[b].rearrange("(p i) k -> p (i k)", i=POS_PER_PART) for b in range(B)]
        out_rows = [
            [out[b].rearrange("(p i) h d -> p (i h d)", i=POS_PER_PART) for b in range(B)]
            for out in (out_0, out_1, out_2)
        ]

        pairs = [(b, m) for b in range(B) for m in range(PAIRS)]
        store_run = {}
        for b in range(B):
            first = 0
            for size in STORE_SIZES[b]:
                for m in range(first // 2, (first + size) // 2):
                    store_run[(b, m)] = (first, size)
                first += size

        w_rows = []

        def load_w(kind):
            w_kind = const.tile([P, GROUPS, E], BF16, name="w_rows_%d" % kind)
            nc.sync.dma_start(
                out=w_kind[:],
                in_=W_qkv.rearrange("(g a p) k -> a p g k", g=GROUPS, p=P)[kind],
            )
            w_rows.append(w_kind)

        x_words = {}

        def load_x(b, first, size):
            x_run = x_pool.tile([P, size * E], BF16, name="x_%d_%d" % (b, first))
            nc.sync.dma_start(out=x_run[:], in_=x_rows[b][:, first * E : (first + size) * E])
            for i in range(size):
                x_words[(b, first + i)] = x_run[:].bitcast(F32)[:, i * WORDS : (i + 1) * WORDS]

        load_w(0)
        load_w(1)
        for b in range(B):
            first = 0
            for size in LOAD_SIZES[b]:
                load_x(b, first, size)
                if b == 0 and first == 0:
                    load_w(2)
                first += size

        w_grouped = const.tile([P, 3 * HD * 4], BF16, align_bytes=64)
        w_words = w_grouped[:].bitcast(F32).rearrange("p (c u) -> p c u", u=2)
        w_codes = const.tile([P, 3 * HD], U32, align_bytes=64)
        w_scales = const.tile([P, 3 * HD], U8, align_bytes=64)

        def transpose_w(kind, tag):
            w_t = psum.tile([P, 2, GROUPS, P], F32, name=tag)
            for g in range(GROUPS):
                words = w_rows[kind][:, g, :].bitcast(F32)
                for u in range(2):
                    nc.tensor.transpose(w_t[:, u, g, :], words[:, u:WORDS:2], identity[:])
            return w_t

        def sort_w(kind, w_t):
            halves = w_t[:].rearrange("p u g (hh f d) -> p f (g hh) d u", hh=2, f=2)
            for f in range(2):
                first = f * HD + kind * (HD // 2)
                nc.scalar.copy(
                    out=w_words[:, first : first + HD // 2, :].rearrange("p (h d) u -> p h d u", h=H),
                    in_=halves[:, f, :, :, :],
                )

        def quantise_w(block):
            columns = slice(block * HD, (block + 1) * HD)
            nc.vector.quantize_mx(
                out=w_codes[:, columns].bitcast(FP8X4),
                scales=w_scales[:, columns],
                in_=w_grouped[:, block * HD * 4 : (block + 1) * HD * 4],
            )

        stage_of = {}

        def transpose_pair(pair, half, grouped):
            b, m = pair
            transposed = psum.tile([P, 2, 2, P], F32, name="transposed")
            for side in range(2):
                words = x_words[(b, 2 * m + side)]
                for u in range(2):
                    nc.tensor.transpose(
                        transposed[:, side, u, :], words[:, u:WORDS:2], identity[:]
                    )
            nc.scalar.copy(
                out=grouped[:, half * 2 * E : (half + 1) * 2 * E]
                .bitcast(F32)
                .rearrange("p (s r u) -> p s r u", s=2, u=2),
                in_=transposed[:].rearrange("p s u r -> p s r u"),
            )

        def quantise_tokens(grouped, codes, scales, first, last):
            nc.vector.quantize_mx(
                out=codes[:, first * P : last * P].bitcast(FP8X4),
                scales=scales[:, first * P : last * P],
                in_=grouped[:, first * E : last * E],
            )

        def new_grouped():
            return operand_pool.tile([P, 4 * E], BF16, align_bytes=64, name="grouped")

        def new_operand():
            codes = operand_pool.tile([P, 4 * P], U32, align_bytes=64)
            scales = operand_pool.tile([P, 4 * P], U8, align_bytes=64)
            return codes, scales

        def multiply_weights(block, half, codes, scales):
            bank = psum.tile([P, 2 * HD], F32, name=("rotated_ps", "passing_ps", "v_ps")[block])
            for side in range(2):
                tokens = slice((2 * half + side) * P, (2 * half + side + 1) * P)
                nc.tensor.matmul_mx(
                    out=bank[:, side * HD : (side + 1) * HD],
                    lhsT=codes[:, tokens].bitcast(FP8X4),
                    lhsT_scale=scales[:, tokens],
                    rhs=w_codes[:, block * HD : (block + 1) * HD].bitcast(FP8X4),
                    rhs_scale=w_scales[:, block * HD : (block + 1) * HD],
                    start=True,
                    stop=True,
                )
            return bank

        def pass_pair(pair, half, codes, scales):
            b, m = pair
            first, size = store_run[pair]
            if 2 * m == first:
                qk_stage = stage_pool.tile([P, 2, MAX_STORE * HD], F32)
                v_stage = stage_pool.tile([P, MAX_STORE * HD], F32)
                stage_of[(b, first)] = (qk_stage, v_stage)
            qk_stage, v_stage = stage_of[(b, first)]
            columns = slice((2 * m - first) * HD, (2 * m - first + 2) * HD)
            qk_out = qk_stage[:, :, columns].rearrange("p c (s h d) -> p c s h d", s=2, h=H)

            passing_ps = multiply_weights(1, half, codes, scales)
            v_ps = multiply_weights(2, half, codes, scales)
            nc.scalar.copy(
                out=qk_out[:, :, :, :, ROT:DH],
                in_=passing_ps[:].rearrange("p (s c h d) -> p c s h d", s=2, c=2, h=H),
            )
            nc.scalar.copy(out=v_stage[:, columns], in_=v_ps[:])
            return qk_out[:, :, :, :, 0:ROT]

        def multiply_pair(pair, rotated_ps, parts):
            products = operand_pool.tile([P, 2, 2 * HD], F32)
            for sides in parts:
                shape = [P, 2, sides.stop - sides.start, 2 * H, ANGLES, 2]
                nc.vector.tensor_tensor(
                    out=products[:].rearrange("p k (s c j e) -> p k s c j e", s=2, c=2 * H, e=2)[
                        :, :, sides, :, :, :
                    ],
                    in0=rotated_ps[:]
                    .rearrange("p (s c j k) -> p k s c j", s=2, c=2 * H, k=2)[:, :, sides, :, :]
                    .unsqueeze(5)
                    .to_broadcast(shape),
                    in1=tables[:, pair[1], :, sides, :]
                    .rearrange("p k s (j e) -> p k s j e", e=2)
                    .unsqueeze(3)
                    .to_broadcast(shape),
                    op=ALU.mult,
                )
            return products

        def add_pair(engine, products, rotated_out, parts):
            terms = products[:].rearrange("p k (s c h d) -> p k c s h d", s=2, c=2, h=H)
            for sides in parts:
                engine.tensor_tensor(
                    out=rotated_out[:, :, sides, :, :],
                    in0=terms[:, 0, :, sides, :, :],
                    in1=terms[:, 1, :, sides, :, :],
                    op=ALU.add,
                )

        def store_if_complete(pair):
            b, m = pair
            first, size = store_run[pair]
            if 2 * m + 2 == first + size:
                qk_stage, v_stage = stage_of[(b, first)]
                columns = slice(first * HD, (first + size) * HD)
                nc.sync.dma_start(out=out_rows[2][b][:, columns], in_=v_stage[:, 0 : size * HD])
                nc.sync.dma_start(out=out_rows[0][b][:, columns], in_=qk_stage[:, 0, 0 : size * HD])
                nc.sync.dma_start(out=out_rows[1][b][:, columns], in_=qk_stage[:, 1, 0 : size * HD])

        warm_in = const.tile([P, 1], F32)
        warm_out = const.tile([P, 1], F32)
        nc.vector.memset(warm_in[:], 0.0)
        nc.scalar.activation(out=warm_out[:], in_=warm_in[:], func=ACT.Sin)
        tables = const.tile([P, PAIRS, 2, 2, ROT], F32)
        coarse, fine = start_rope_tables(nc, const)
        identity = const.tile([P, P], F32)
        make_identity(nc, identity[:])

        quads = [pairs[n : n + 2] for n in range(0, len(pairs), 2)]
        last_round = len(quads) - 1
        whole = [slice(0, 2)]
        halves = [slice(0, 1), slice(1, 2)]
        grouped_of = {0: new_grouped(), 1: new_grouped()}
        rotated_of = {}

        for kind, tag in ((0, "passing_ps"), (1, "v_ps")):
            sort_w(kind, transpose_w(kind, tag))
        transpose_pair(quads[0][0], 0, grouped_of[0])
        early, late = rope_arguments(nc, const, coarse, fine, ((0, 2), (2, PAIRS)))
        finish_rope_tables(nc, tables, early, 0, 2)
        w_v = transpose_w(2, "rotated_ps")
        transpose_pair(quads[0][1], 1, grouped_of[0])
        nc.scalar.copy(
            out=w_words[:, 2 * HD : 3 * HD, :], in_=w_v[:].rearrange("p u g r -> p (g r) u")
        )
        for half in range(2):
            transpose_pair(quads[1][half], half, grouped_of[1])
        codes, scales = new_operand()
        quantise_w(0)
        quantise_tokens(grouped_of[0], codes, scales, 0, 2)
        rotated_a = multiply_weights(0, 0, codes, scales)
        quantise_w(1)
        quantise_tokens(grouped_of[0], codes, scales, 2, 4)
        quantise_w(2)
        rotated_of[quads[0][0]] = (rotated_a, pass_pair(quads[0][0], 0, codes, scales))
        rotated_out = pass_pair(quads[0][1], 1, codes, scales)
        rotated_of[quads[0][1]] = (multiply_weights(0, 1, codes, scales), rotated_out)
        finish_rope_tables(nc, tables, late, 2, PAIRS)

        for r in range(len(quads)):
            pair_a, pair_b = quads[r]
            products_a = multiply_pair(pair_a, rotated_of[pair_a][0], whole)
            if r + 2 <= last_round:
                grouped_of[r + 2] = new_grouped()
                for half in range(2):
                    transpose_pair(quads[r + 2][half], half, grouped_of[r + 2])
            if r + 1 <= last_round:
                codes, scales = new_operand()
                quantise_tokens(grouped_of[r + 1], codes, scales, 0, 4)
            add_pair(nc.vector, products_a, rotated_of[pair_a][1], whole)
            store_if_complete(pair_a)
            if r + 1 <= last_round:
                next_a, next_b = quads[r + 1]
                rotated_a = multiply_weights(0, 0, codes, scales)
                rotated_of[next_a] = (rotated_a, pass_pair(next_a, 0, codes, scales))
                rotated_out = pass_pair(next_b, 1, codes, scales)
            products_b = multiply_pair(pair_b, rotated_of[pair_b][0], halves)
            engine = nc.vector if r == last_round else nc.gpsimd
            add_pair(engine, products_b, rotated_of[pair_b][1], halves)
            store_if_complete(pair_b)
            if r + 1 <= last_round:
                rotated_of[next_b] = (multiply_weights(0, 1, codes, scales), rotated_out)
